import numpy as np
import ml_dtypes


def mxq(x, axis, fmt="e4m3"):
    dtype, down = {"e4m3": (ml_dtypes.float8_e4m3fn, 7), "e5m2": (ml_dtypes.float8_e5m2, 14)}[fmt]
    v = np.moveaxis(np.asarray(x, np.float32).astype(ml_dtypes.bfloat16).astype(np.float64), axis, -1)
    blocks = v.reshape(v.shape[:-1] + (-1, 32))
    amax = np.abs(blocks).max(-1, keepdims=True)
    byte = np.maximum(np.where(amax > 0, np.frexp(amax)[1] - 1 + 127, 0) - down, 1)
    scale = np.exp2(byte - 127.0)
    codes = (blocks / scale).astype(np.float32).astype(dtype).astype(np.float64)
    return np.moveaxis((codes * scale).reshape(v.shape), -1, axis)


WIDE = False


def mx_kscale(k):
    if not WIDE:
        return np.ones(k)
    levels = np.array([10, -10, 5, -5, 0])
    a = np.random.permutation(np.resize(levels, k // 512 * 4)).reshape(k // 512, 4)
    idx = np.arange(k)
    return np.exp2(a[idx // 512, idx % 128 // 32])


BF16 = ml_dtypes.bfloat16


def bf(x):
    return np.asarray(x, np.float32).astype(BF16)


def f64(x):
    return np.asarray(x).astype(np.float64)


B, S, H, D = 8, 512, 2, 256


def setup_inputs():
    s = mx_kscale(S)
    bias = np.random.standard_normal((1, 1, S, S)) + np.log(s)
    shut = np.random.random((1, 1, S, S)) < 0.125
    return {"q": bf(np.random.standard_normal((B, S, H, D))),
            "k": bf(np.random.standard_normal((B, S, H, D))),
            "v": bf(np.random.standard_normal((B, S, H, D)) * (np.sqrt(S) / 8.0) * s.mean() / s[None, :, None, None]),
            "start_pos": 0, "seqlen": S,
            "mask": bf(np.where(shut, -1e9, bias))}


def reference(q, k, v, start_pos, seqlen, mask):
    qs = f64(q).transpose(0, 2, 1, 3)
    ks = f64(k).transpose(0, 2, 1, 3)
    vs = f64(v).transpose(0, 2, 1, 3)
    scores = qs @ ks.transpose(0, 1, 3, 2) / np.sqrt(D)
    scores = scores + f64(mask)
    e = np.exp(scores - scores.max(-1, keepdims=True))
    out = (mxq(e, 3, "e4m3") @ mxq(vs, 2, "e4m3")) / e.sum(-1, keepdims=True)
    return out.transpose(0, 2, 1, 3)

@@ -1,0 +1,309 @@
+from contextlib import ExitStack
+
+import concourse.bass as bass
+import concourse.mybir as mybir
+import concourse.tile as tile
+from concourse.masks import make_identity
+
+F32 = mybir.dt.float32
+BF16 = mybir.dt.bfloat16
+U32 = mybir.dt.uint32
+U8 = mybir.dt.uint8
+FP8X4 = mybir.dt.float8_e4m3fn_x4
+ALU = mybir.AluOpType
+ACTF = mybir.ActivationFunctionType
+AX = mybir.AxisListType
+
+B, S, H, D = 8, 512, 2, 256
+P = 128
+NT = S // P
+NS = B * NT
+FLOPS = 2 * (2 * B * H * S * S * D)
+
+MANUAL = True
+E_REGROUP = "pool"
+V_REGROUP = "pool"
+
+
+def tile_attention_gear_t_kernel(tc, q, k, v, start_pos, seqlen, mask, out):
+    nc = tc.nc
+    with ExitStack() as ctx:
+        if MANUAL:
+            ctx.enter_context(tc.manual_schedule())
+        const = ctx.enter_context(tc.tile_pool(name="const", bufs=1))
+        raw = ctx.enter_context(tc.tile_pool(name="raw", bufs=2))
+        tp = ctx.enter_context(tc.tile_pool(name="tp", bufs=2))
+        work = ctx.enter_context(tc.tile_pool(name="work", bufs=2))
+        small = ctx.enter_context(tc.tile_pool(name="small", bufs=3))
+        ps_s = ctx.enter_context(tc.psum_pool(name="ps_s", bufs=4))
+        ps_t = ctx.enter_context(tc.psum_pool(name="ps_t", bufs=1))
+        ps_e = ctx.enter_context(tc.psum_pool(name="ps_e", bufs=2))
+        ps_o = ctx.enter_context(tc.psum_pool(name="ps_o", bufs=1))
+
+        st = {}
+
+        def load_kq(b):
+            k_raw = raw.tile([P, NT, H * D], BF16, tag="k_raw")
+            nc.sync.dma_start(out=k_raw[:], in_=k[b].rearrange("(t p) h d -> p t (h d)", p=P))
+            q_raw = raw.tile([P, NT, H * D], BF16, tag="q_raw")
+            nc.sync.dma_start(out=q_raw[:], in_=q[b].rearrange("(p j) h d -> p j (h d)", j=NT))
+            st[("k_raw", b)] = k_raw
+            st[("q_raw", b)] = q_raw
+
+        def load_v(b):
+            v_raw = raw.tile([P, NT, H * D], BF16, tag="v_raw", bufs=3)
+            nc.sync.dma_start(out=v_raw[:], in_=v[b].rearrange("(t p) h d -> p t (h d)", p=P))
+            st[("v_raw", b)] = v_raw
+
+        load_kq(0)
+        mask_sb = const.tile([P, NT, S], BF16, name="mask_sb")
+        nc.sync.dma_start(out=mask_sb[:], in_=mask[0, 0].rearrange("(p j) c -> p j c", j=NT))
+        load_kq(1)
+        load_v(0)
+        load_v(1)
+
+        ident_f = const.tile([P, P], F32, name="ident_f")
+        make_identity(nc, ident_f[:])
+        ident_b = const.tile([P, P], BF16, name="ident_b")
+        make_identity(nc, ident_b[:])
+        warm = const.tile([P, 1], F32, name="warm")
+        nc.vector.memset(warm[:], 0.0)
+        nc.scalar.activation(out=warm[:], in_=warm[:], func=ACTF.Exp)
+
+        def prep_t(b, r, pool, tag):
+            which = "k" if r < 2 else "q"
+            h = r % 2
+            src = st[(which + "_raw", b)]
+            pt = pool.tile([P, S], F32, tag=tag, name="pt")
+            words = src[:].bitcast(F32)
+            for i in range(NT):
+                nc.tensor.transpose(
+                    out=pt[:, i * P:(i + 1) * P],
+                    in_=words[:, i, h * P:(h + 1) * P],
+                    identity=ident_f[:],
+                )
+            st[("pt", b, r)] = pt
+
+        def prep_evac(b, r, eng):
+            which = "k" if r < 2 else "q"
+            h = r % 2
+            dst = tp.tile([P, S], F32, tag="%sT%d" % (which, h), name="dstT")
+            pt = st[("pt", b, r)]
+            if eng == "act":
+                nc.scalar.copy(out=dst[:], in_=pt[:])
+            else:
+                nc.vector.tensor_copy(out=dst[:], in_=pt[:])
+            st[(which + "T", b, h)] = dst[:].bitcast(BF16).rearrange("p (s e) -> p s e", e=2)
+
+        def qk(n, hh):
+            b, j = divmod(n, NT)
+            ps = ps_s.tile([P, S], F32, tag="s", name="ps")
+            qT = st[("qT", b, hh)]
+            kT = st[("kT", b, hh)]
+            for e in range(2):
+                nc.tensor.matmul(
+                    out=ps[:],
+                    lhsT=qT[:, j * P:(j + 1) * P, e],
+                    rhs=kT[:, :, e],
+                    start=(e == 0),
+                    stop=(e == 1),
+                )
+            st[("ps", n, hh)] = ps
+
+        def stt(n, hh):
+            b, j = divmod(n, NT)
+            if hh == 0:
+                st[("s2", n)] = work.tile([P, H, S], F32, tag="s2", name="s2", bufs=3)
+            s2 = st[("s2", n)]
+            nc.vector.scalar_tensor_tensor(
+                out=s2[:, hh, :],
+                in0=st[("ps", n, hh)][:],
+                scalar=-1.0 / 16.0,
+                in1=mask_sb[:, j, :],
+                op0=ALU.mult,
+                op1=ALU.subtract,
+            )
+
+        def rowmin(n):
+            negm = small.tile([P, H], F32, tag="negm", name="negm")
+            nc.vector.tensor_reduce(out=negm[:], in_=st[("s2", n)][:], axis=AX.X, op=ALU.min)
+            st[("negm", n)] = negm
+
+        def expo(n, hh):
+            if hh == 0:
+                st[("e2", n)] = work.tile([P, H, S], BF16, tag="e2", name="e2")
+                st[("rs", n)] = small.tile([P, H], F32, tag="rs", name="rs", bufs=4)
+            nc.scalar.activation(
+                out=st[("e2", n)][:, hh, :],
+                in_=st[("s2", n)][:, hh, :],
+                func=ACTF.Exp,
+                bias=st[("negm", n)][:, hh:hh + 1],
+                scale=-1.0,
+                accum_out=st[("rs", n)][:, hh:hh + 1],
+            )
+
+        def e_t(n, hh):
+            if hh == 0:
+                st[("pe", n)] = ps_e.tile([P, NT, H, P], BF16, tag="pe", name="pe")
+            pe = st[("pe", n)]
+            e2 = st[("e2", n)]
+            for t in range(NT):
+                nc.tensor.transpose(
+                    out=pe[:, t, hh, :],
+                    in_=e2[:, hh, t * P:(t + 1) * P],
+                    identity=ident_b[:],
+                )
+
+        def evac_t(n):
+            epl = work.tile([P, NT, H * P], BF16, tag="epl", name="epl")
+            nc.scalar.copy(
+                out=epl[:].rearrange("p t c -> p (t c)"),
+                in_=st[("pe", n)][:].rearrange("p t h c -> p (t h c)"),
+            )
+            st[("epl", n)] = epl
+
+        def regroup(dst, src, eng):
+            if eng == "pool":
+                nc.gpsimd.tensor_scalar(
+                    out=dst,
+                    in0=src.rearrange("p t c -> p c t"),
+                    scalar1=1.0,
+                    scalar2=0.0,
+                    op0=ALU.mult,
+                    op1=ALU.add,
+                )
+            else:
+                nc.vector.tensor_copy(
+                    out=dst.rearrange("p (c i) t -> p c t i", i=4),
+                    in_=src.rearrange("p t (c i) -> p c t i", i=4),
+                )
+
+        def regroup_e(n):
+            grp = work.tile([P, H * P, NT], BF16, tag="grp", name="grp", align_bytes=64)
+            regroup(grp[:], st[("epl", n)][:], E_REGROUP)
+            st[("grp", n)] = grp
+
+        def quant_e(n):
+            ec = work.tile([P, H * P], U32, tag="ec", name="ec", align_bytes=64)
+            es = work.tile([P, H * P], U8, tag="es", name="es", align_bytes=64)
+            nc.vector.quantize_mx(
+                out=ec[:].bitcast(FP8X4),
+                scales=es[:],
+                in_=st[("grp", n)][:].rearrange("p c t -> p (c t)"),
+            )
+            rc = small.tile([P, H], F32, tag="rc", name="rc")
+            nc.vector.reciprocal(out=rc[:], in_=st[("rs", n)][:])
+            st[("ec", n)] = ec
+            st[("es", n)] = es
+            st[("rc", n)] = rc
+
+        def regroup_v(b, r):
+            if r == 0:
+                st[("vgrp", b)] = work.tile([P, H * D, NT], BF16, tag="vgrp", name="vgrp", align_bytes=64)
+            cs = slice(r * P, (r + 1) * P)
+            regroup(st[("vgrp", b)][:, cs, :], st[("v_raw", b)][:, :, cs], V_REGROUP)
+
+        def quant_v(b):
+            vc = work.tile([P, H * D], U32, tag="vc", name="vc", align_bytes=64)
+            vs = work.tile([P, H * D], U8, tag="vs", name="vs", align_bytes=64)
+            nc.vector.quantize_mx(
+                out=vc[:].bitcast(FP8X4),
+                scales=vs[:],
+                in_=st[("vgrp", b)][:].rearrange("p c t -> p (c t)"),
+            )
+            st[("vc", b)] = vc
+            st[("vs", b)] = vs
+
+        def pv(n):
+            b, j = divmod(n, NT)
+            po = ps_o.tile([P, H, D], F32, tag="po", name="po")
+            for hh in range(H):
+                nc.tensor.matmul_mx(
+                    out=po[:, hh, :],
+                    lhsT=st[("ec", n)][:, hh * P:(hh + 1) * P].bitcast(FP8X4),
+                    lhsT_scale=st[("es", n)][:, hh * P:(hh + 1) * P],
+                    rhs=st[("vc", b)][:, hh * D:(hh + 1) * D].bitcast(FP8X4),
+                    rhs_scale=st[("vs", b)][:, hh * D:(hh + 1) * D],
+                    start=True,
+                    stop=True,
+                )
+            st[("po", n)] = po
+
+        def o_evac(n):
+            ob = work.tile([P, H, D], F32, tag="ob", name="ob", bufs=4)
+            for hh in range(H):
+                nc.scalar.activation(
+                    out=ob[:, hh, :],
+                    in_=st[("po", n)][:, hh, :],
+                    func=ACTF.Copy,
+                    scale=st[("rc", n)][:, hh:hh + 1],
+                )
+            st[("ob", n)] = ob
+
+        def store(n):
+            b, j = divmod(n, NT)
+            nc.sync.dma_start(
+                out=out[b].rearrange("(p j) h d -> p j (h d)", j=NT)[:, j, :],
+                in_=st[("ob", n)][:].rearrange("p h d -> p (h d)"),
+            )
+
+        for r in range(4):
+            prep_t(0, r, ps_s, "s")
+        for r in range(4):
+            prep_evac(0, r, "act" if r % 2 == 0 else "dve")
+
+        def ok(n):
+            return 0 <= n < NS
+
+        def preps(c):
+            if c in (0, 1):
+                return [(1, 2 * c), (1, 2 * c + 1)]
+            x = c + 2
+            b1 = x // 4 + 1
+            if c >= 2 and b1 < B:
+                return [(b1, x % 4)]
+            return []
+
+        for c in range(-2, NS + 2):
+            pl = preps(c)
+            if ok(c - 2):
+                if (c - 2) % NT == 0:
+                    quant_v((c - 2) // NT)
+                quant_e(c - 2)
+                pv(c - 2)
+            if ok(c):
+                expo(c, 0)
+                e_t(c, 0)
+            if ok(c - 1):
+                evac_t(c - 1)
+                regroup_e(c - 1)
+            xb, xr = divmod(c + 2, NT)
+            if xb < B:
+                regroup_v(xb, xr)
+            if ok(c + 2):
+                qk(c + 2, 0)
+            if ok(c + 1):
+                stt(c + 1, 0)
+            if pl:
+                prep_t(pl[0][0], pl[0][1], ps_t, "t")
+            if ok(c):
+                expo(c, 1)
+                e_t(c, 1)
+            if ok(c + 2):
+                qk(c + 2, 1)
+            if ok(c + 1):
+                stt(c + 1, 1)
+                rowmin(c + 1)
+            if pl:
+                prep_evac(pl[0][0], pl[0][1], "act")
+            if ok(c - 2):
+                o_evac(c - 2)
+                store(c - 2)
+            if len(pl) > 1:
+                prep_t(pl[1][0], pl[1][1], ps_t, "t")
+                prep_evac(pl[1][0], pl[1][1], "act")
+            if (c + 2) % NT == 0:
+                nb = (c + 2) // NT + 2
+                if nb < B:
+                    load_kq(nb)
+                    load_v(nb)

@@ -37,8 +37,8 @@ def tile_attention_gear_t_kernel(tc, q, k, v, start_pos, seqlen, mask, out):
         small = ctx.enter_context(tc.tile_pool(name="small", bufs=3))
         ps_s = ctx.enter_context(tc.psum_pool(name="ps_s", bufs=4))
         ps_t = ctx.enter_context(tc.psum_pool(name="ps_t", bufs=1))
-        ps_e = ctx.enter_context(tc.psum_pool(name="ps_e", bufs=2))
-        ps_o = ctx.enter_context(tc.psum_pool(name="ps_o", bufs=1))
+        ps_e = ctx.enter_context(tc.psum_pool(name="ps_e", bufs=1))
+        ps_o = ctx.enter_context(tc.psum_pool(name="ps_o", bufs=2))
 
         st = {}
 
@@ -132,7 +132,7 @@ def tile_attention_gear_t_kernel(tc, q, k, v, start_pos, seqlen, mask, out):
         def expo(n, hh):
             if hh == 0:
                 st[("e2", n)] = work.tile([P, H, S], BF16, tag="e2", name="e2")
-                st[("rs", n)] = small.tile([P, H], F32, tag="rs", name="rs", bufs=4)
+                st[("rs", n)] = small.tile([P, H], F32, tag="rs", name="rs", bufs=5)
             nc.scalar.activation(
                 out=st[("e2", n)][:, hh, :],
                 in_=st[("s2", n)][:, hh, :],
@@ -179,7 +179,7 @@ def tile_attention_gear_t_kernel(tc, q, k, v, start_pos, seqlen, mask, out):
                 )
 
         def regroup_e(n):
-            grp = work.tile([P, H * P, NT], BF16, tag="grp", name="grp", align_bytes=64)
+            grp = work.tile([P, H * P, NT], BF16, tag="grp", name="grp", bufs=3, align_bytes=64)
             regroup(grp[:], st[("epl", n)][:], E_REGROUP)
             st[("grp", n)] = grp
 
@@ -264,16 +264,19 @@ def tile_attention_gear_t_kernel(tc, q, k, v, start_pos, seqlen, mask, out):
                 return [(b1, x % 4)]
             return []
 
-        for c in range(-2, NS + 2):
+        LAG = 3
+        for c in range(-2, NS + LAG):
             pl = preps(c)
-            if ok(c - 2):
-                if (c - 2) % NT == 0:
-                    quant_v((c - 2) // NT)
-                quant_e(c - 2)
-                pv(c - 2)
-            if ok(c):
-                expo(c, 0)
-                e_t(c, 0)
+            if ok(c - LAG):
+                if (c - LAG) % NT == 0:
+                    quant_v((c - LAG) // NT)
+                quant_e(c - LAG)
+                pv(c - LAG)
+            for i, u in enumerate(pl):
+                if i == 0:
+                    prep_t(u[0], u[1], ps_t, "t")
+                else:
+                    prep_t(u[0], u[1], ps_o, "po")
             if ok(c - 1):
                 evac_t(c - 1)
                 regroup_e(c - 1)
@@ -284,24 +287,22 @@ def tile_attention_gear_t_kernel(tc, q, k, v, start_pos, seqlen, mask, out):
                 qk(c + 2, 0)
             if ok(c + 1):
                 stt(c + 1, 0)
-            if pl:
-                prep_t(pl[0][0], pl[0][1], ps_t, "t")
             if ok(c):
-                expo(c, 1)
-                e_t(c, 1)
+                expo(c, 0)
+                e_t(c, 0)
             if ok(c + 2):
                 qk(c + 2, 1)
             if ok(c + 1):
                 stt(c + 1, 1)
                 rowmin(c + 1)
-            if pl:
-                prep_evac(pl[0][0], pl[0][1], "act")
-            if ok(c - 2):
-                o_evac(c - 2)
-                store(c - 2)
-            if len(pl) > 1:
-                prep_t(pl[1][0], pl[1][1], ps_t, "t")
-                prep_evac(pl[1][0], pl[1][1], "act")
+            if ok(c):
+                expo(c, 1)
+                e_t(c, 1)
+            for u in pl:
+                prep_evac(u[0], u[1], "act")
+            if ok(c - LAG):
+                o_evac(c - LAG)
+                store(c - LAG)
             if (c + 2) % NT == 0:
                 nb = (c + 2) // NT + 2
                 if nb < B:

@@ -66,6 +66,8 @@ def tile_attention_gear_t_kernel(tc, q, k, v, start_pos, seqlen, mask, out):
         make_identity(nc, ident_f[:])
         ident_b = const.tile([P, P], BF16, name="ident_b")
         make_identity(nc, ident_b[:])
+        ident16 = const.tile([P, P], BF16, name="ident16")
+        nc.gpsimd.tensor_scalar(out=ident16[:], in0=ident_b[:], scalar1=16.0, scalar2=0.0, op0=ALU.mult, op1=ALU.add)
         warm = const.tile([P, 1], F32, name="warm")
         nc.vector.memset(warm[:], 0.0)
         nc.scalar.activation(out=warm[:], in_=warm[:], func=ACTF.Exp)
@@ -95,26 +97,44 @@ def tile_attention_gear_t_kernel(tc, q, k, v, start_pos, seqlen, mask, out):
                 nc.vector.tensor_copy(out=dst[:], in_=pt[:])
             st[(which + "T", b, h)] = dst[:].bitcast(BF16).rearrange("p (s e) -> p s e", e=2)
 
+        def pe_mask(n, hh):
+            return hh == 0 and (3 * n) % 8 < 3
+
         def qk(n, hh):
             b, j = divmod(n, NT)
             ps = ps_s.tile([P, S], F32, tag="s", name="ps")
             qT = st[("qT", b, hh)]
             kT = st[("kT", b, hh)]
+            on_pe = pe_mask(n, hh)
             for e in range(2):
                 nc.tensor.matmul(
                     out=ps[:],
                     lhsT=qT[:, j * P:(j + 1) * P, e],
                     rhs=kT[:, :, e],
                     start=(e == 0),
-                    stop=(e == 1),
+                    stop=(e == 1 and not on_pe),
                 )
+            if on_pe:
+                nc.tensor.matmul(out=ps[:], lhsT=ident16[:], rhs=mask_sb[:, j, :], start=False, stop=True)
             st[("ps", n, hh)] = ps
 
         def stt(n, hh):
             b, j = divmod(n, NT)
             if hh == 0:
                 st[("s2", n)] = work.tile([P, H, S], F32, tag="s2", name="s2", bufs=3)
+                st[("negm", n)] = small.tile([P, H], F32, tag="negm", name="negm")
             s2 = st[("s2", n)]
+            if pe_mask(n, hh):
+                nc.vector.tensor_scalar(
+                    out=s2[:, hh, :],
+                    in0=st[("ps", n, hh)][:],
+                    scalar1=-1.0 / 16.0,
+                    scalar2=None,
+                    op0=ALU.mult,
+                    op1=ALU.min,
+                    accum_out=st[("negm", n)][:, hh:hh + 1],
+                )
+                return
             nc.vector.scalar_tensor_tensor(
                 out=s2[:, hh, :],
                 in0=st[("ps", n, hh)][:],
@@ -125,9 +145,11 @@ def tile_attention_gear_t_kernel(tc, q, k, v, start_pos, seqlen, mask, out):
             )
 
         def rowmin(n):
-            negm = small.tile([P, H], F32, tag="negm", name="negm")
-            nc.vector.tensor_reduce(out=negm[:], in_=st[("s2", n)][:], axis=AX.X, op=ALU.min)
-            st[("negm", n)] = negm
+            negm = st[("negm", n)]
+            if pe_mask(n, 0):
+                nc.vector.tensor_reduce(out=negm[:, 1:2], in_=st[("s2", n)][:, 1, :], axis=AX.X, op=ALU.min)
+            else:
+                nc.vector.tensor_reduce(out=negm[:], in_=st[("s2", n)][:], axis=AX.X, op=ALU.min)
 
         def expo(n, hh):
             if hh == 0:
@@ -179,7 +201,7 @@ def tile_attention_gear_t_kernel(tc, q, k, v, start_pos, seqlen, mask, out):
                 )
 
         def regroup_e(n):
-            grp = work.tile([P, H * P, NT], BF16, tag="grp", name="grp", bufs=3, align_bytes=64)
+            grp = work.tile([P, H * P, NT], BF16, tag="grp", name="grp", bufs=2, align_bytes=64)
             regroup(grp[:], st[("epl", n)][:], E_REGROUP)
             st[("grp", n)] = grp
 

@@ -21,6 +21,7 @@ NS = B * NT
 FLOPS = 2 * (2 * B * H * S * S * D)
 
 MANUAL = True
+NLAST = 2
 E_REGROUP = "pool"
 V_REGROUP = "pool"
 
@@ -37,8 +38,8 @@ def tile_attention_gear_t_kernel(tc, q, k, v, start_pos, seqlen, mask, out):
         small = ctx.enter_context(tc.tile_pool(name="small", bufs=3))
         ps_s = ctx.enter_context(tc.psum_pool(name="ps_s", bufs=4))
         ps_t = ctx.enter_context(tc.psum_pool(name="ps_t", bufs=1))
-        ps_e = ctx.enter_context(tc.psum_pool(name="ps_e", bufs=1))
-        ps_o = ctx.enter_context(tc.psum_pool(name="ps_o", bufs=2))
+        ps_e = ctx.enter_context(tc.psum_pool(name="ps_e", bufs=2))
+        ps_o = ctx.enter_context(tc.psum_pool(name="ps_o", bufs=1))
 
         st = {}
 
@@ -205,6 +206,11 @@ def tile_attention_gear_t_kernel(tc, q, k, v, start_pos, seqlen, mask, out):
             regroup(grp[:], st[("epl", n)][:], E_REGROUP)
             st[("grp", n)] = grp
 
+        def evac_regroup_e(n):
+            grp = work.tile([P, H * P, NT], BF16, tag="grp", name="grp", bufs=2, align_bytes=64)
+            nc.vector.tensor_copy(out=grp[:], in_=st[("pe", n)][:].rearrange("p t h c -> p (h c) t"))
+            st[("grp", n)] = grp
+
         def quant_e(n):
             ec = work.tile([P, H * P], U32, tag="ec", name="ec", align_bytes=64)
             es = work.tile([P, H * P], U8, tag="es", name="es", align_bytes=64)
@@ -238,7 +244,10 @@ def tile_attention_gear_t_kernel(tc, q, k, v, start_pos, seqlen, mask, out):
 
         def pv(n):
             b, j = divmod(n, NT)
-            po = ps_o.tile([P, H, D], F32, tag="po", name="po")
+            if n >= NS - NLAST:
+                po = ps_s.tile([P, H, D], F32, tag="s", name="po")
+            else:
+                po = ps_o.tile([P, H, D], F32, tag="po", name="po")
             for hh in range(H):
                 nc.tensor.matmul_mx(
                     out=po[:, hh, :],
@@ -289,29 +298,32 @@ def tile_attention_gear_t_kernel(tc, q, k, v, start_pos, seqlen, mask, out):
         LAG = 3
         for c in range(-2, NS + LAG):
             pl = preps(c)
-            if ok(c - LAG):
-                if (c - LAG) % NT == 0:
-                    quant_v((c - LAG) // NT)
-                quant_e(c - LAG)
-                pv(c - LAG)
             for i, u in enumerate(pl):
                 if i == 0:
                     prep_t(u[0], u[1], ps_t, "t")
                 else:
                     prep_t(u[0], u[1], ps_o, "po")
-            if ok(c - 1):
-                evac_t(c - 1)
-                regroup_e(c - 1)
-            xb, xr = divmod(c + 2, NT)
-            if xb < B:
-                regroup_v(xb, xr)
             if ok(c + 2):
                 qk(c + 2, 0)
             if ok(c + 1):
                 stt(c + 1, 0)
+            if ok(c - LAG):
+                if (c - LAG) % NT == 0:
+                    quant_v((c - LAG) // NT)
+                quant_e(c - LAG)
+                pv(c - LAG)
             if ok(c):
                 expo(c, 0)
                 e_t(c, 0)
+            if ok(c - 1):
+                if c - 1 >= NS - NLAST:
+                    evac_regroup_e(c - 1)
+                else:
+                    evac_t(c - 1)
+                    regroup_e(c - 1)
+            xb, xr = divmod(c + 2, NT)
+            if xb < B:
+                regroup_v(xb, xr)
             if ok(c + 2):
                 qk(c + 2, 1)
             if ok(c + 1):

@@ -202,12 +202,12 @@ def tile_attention_gear_t_kernel(tc, q, k, v, start_pos, seqlen, mask, out):
                 )
 
         def regroup_e(n):
-            grp = work.tile([P, H * P, NT], BF16, tag="grp", name="grp", bufs=2, align_bytes=64)
+            grp = work.tile([P, H * P, NT], BF16, tag="grp", name="grp", bufs=3, align_bytes=64)
             regroup(grp[:], st[("epl", n)][:], E_REGROUP)
             st[("grp", n)] = grp
 
         def evac_regroup_e(n):
-            grp = work.tile([P, H * P, NT], BF16, tag="grp", name="grp", bufs=2, align_bytes=64)
+            grp = work.tile([P, H * P, NT], BF16, tag="grp", name="grp", bufs=3, align_bytes=64)
             nc.vector.tensor_copy(out=grp[:], in_=st[("pe", n)][:].rearrange("p t h c -> p (h c) t"))
             st[("grp", n)] = grp
 

from contextlib import ExitStack

import concourse.bass as bass
import concourse.mybir as mybir
import concourse.tile as tile
from concourse.masks import make_identity

F32 = mybir.dt.float32
BF16 = mybir.dt.bfloat16
U32 = mybir.dt.uint32
U8 = mybir.dt.uint8
FP8X4 = mybir.dt.float8_e4m3fn_x4
ALU = mybir.AluOpType
ACTF = mybir.ActivationFunctionType
AX = mybir.AxisListType

B, S, H, D = 8, 512, 2, 256
P = 128
NT = S // P
NS = B * NT
FLOPS = 2 * (2 * B * H * S * S * D)

MANUAL = True
NLAST = 2
E_REGROUP = "pool"
V_REGROUP = "pool"


def tile_attention_gear_t_kernel(tc, q, k, v, start_pos, seqlen, mask, out):
    nc = tc.nc
    with ExitStack() as ctx:
        if MANUAL:
            ctx.enter_context(tc.manual_schedule())
        const = ctx.enter_context(tc.tile_pool(name="const", bufs=1))
        raw = ctx.enter_context(tc.tile_pool(name="raw", bufs=2))
        tp = ctx.enter_context(tc.tile_pool(name="tp", bufs=2))
        work = ctx.enter_context(tc.tile_pool(name="work", bufs=2))
        small = ctx.enter_context(tc.tile_pool(name="small", bufs=3))
        ps_s = ctx.enter_context(tc.psum_pool(name="ps_s", bufs=4))
        ps_t = ctx.enter_context(tc.psum_pool(name="ps_t", bufs=1))
        ps_e = ctx.enter_context(tc.psum_pool(name="ps_e", bufs=2))
        ps_o = ctx.enter_context(tc.psum_pool(name="ps_o", bufs=1))

        st = {}

        def load_kq(b):
            k_raw = raw.tile([P, NT, H * D], BF16, tag="k_raw")
            nc.sync.dma_start(out=k_raw[:], in_=k[b].rearrange("(t p) h d -> p t (h d)", p=P))
            q_raw = raw.tile([P, NT, H * D], BF16, tag="q_raw")
            nc.sync.dma_start(out=q_raw[:], in_=q[b].rearrange("(p j) h d -> p j (h d)", j=NT))
            st[("k_raw", b)] = k_raw
            st[("q_raw", b)] = q_raw

        def load_v(b):
            v_raw = raw.tile([P, NT, H * D], BF16, tag="v_raw", bufs=3)
            nc.sync.dma_start(out=v_raw[:], in_=v[b].rearrange("(t p) h d -> p t (h d)", p=P))
            st[("v_raw", b)] = v_raw

        load_kq(0)
        mask_sb = const.tile([P, NT, S], BF16, name="mask_sb")
        nc.sync.dma_start(out=mask_sb[:], in_=mask[0, 0].rearrange("(p j) c -> p j c", j=NT))
        load_kq(1)
        load_v(0)
        load_v(1)

        ident_f = const.tile([P, P], F32, name="ident_f")
        make_identity(nc, ident_f[:])
        ident_b = const.tile([P, P], BF16, name="ident_b")
        make_identity(nc, ident_b[:])
        ident16 = const.tile([P, P], BF16, name="ident16")
        nc.gpsimd.tensor_scalar(out=ident16[:], in0=ident_b[:], scalar1=16.0, scalar2=0.0, op0=ALU.mult, op1=ALU.add)
        warm = const.tile([P, 1], F32, name="warm")
        nc.vector.memset(warm[:], 0.0)
        nc.scalar.activation(out=warm[:], in_=warm[:], func=ACTF.Exp)

        def prep_t(b, r, pool, tag):
            which = "k" if r < 2 else "q"
            h = r % 2
            src = st[(which + "_raw", b)]
            pt = pool.tile([P, S], F32, tag=tag, name="pt")
            words = src[:].bitcast(F32)
            for i in range(NT):
                nc.tensor.transpose(
                    out=pt[:, i * P:(i + 1) * P],
                    in_=words[:, i, h * P:(h + 1) * P],
                    identity=ident_f[:],
                )
            st[("pt", b, r)] = pt

        def prep_evac(b, r, eng):
            which = "k" if r < 2 else "q"
            h = r % 2
            dst = tp.tile([P, S], F32, tag="%sT%d" % (which, h), name="dstT")
            pt = st[("pt", b, r)]
            if eng == "act":
                nc.scalar.copy(out=dst[:], in_=pt[:])
            else:
                nc.vector.tensor_copy(out=dst[:], in_=pt[:])
            st[(which + "T", b, h)] = dst[:].bitcast(BF16).rearrange("p (s e) -> p s e", e=2)

        def pe_mask(n, hh):
            return hh == 0 and (3 * n) % 8 < 3

        def qk(n, hh):
            b, j = divmod(n, NT)
            ps = ps_s.tile([P, S], F32, tag="s", name="ps")
            qT = st[("qT", b, hh)]
            kT = st[("kT", b, hh)]
            on_pe = pe_mask(n, hh)
            for e in range(2):
                nc.tensor.matmul(
                    out=ps[:],
                    lhsT=qT[:, j * P:(j + 1) * P, e],
                    rhs=kT[:, :, e],
                    start=(e == 0),
                    stop=(e == 1 and not on_pe),
                )
            if on_pe:
                nc.tensor.matmul(out=ps[:], lhsT=ident16[:], rhs=mask_sb[:, j, :], start=False, stop=True)
            st[("ps", n, hh)] = ps

        def stt(n, hh):
            b, j = divmod(n, NT)
            if hh == 0:
                st[("s2", n)] = work.tile([P, H, S], F32, tag="s2", name="s2", bufs=3)
                st[("negm", n)] = small.tile([P, H], F32, tag="negm", name="negm")
            s2 = st[("s2", n)]
            if pe_mask(n, hh):
                nc.vector.tensor_scalar(
                    out=s2[:, hh, :],
                    in0=st[("ps", n, hh)][:],
                    scalar1=-1.0 / 16.0,
                    scalar2=None,
                    op0=ALU.mult,
                    op1=ALU.min,
                    accum_out=st[("negm", n)][:, hh:hh + 1],
                )
                return
            nc.vector.scalar_tensor_tensor(
                out=s2[:, hh, :],
                in0=st[("ps", n, hh)][:],
                scalar=-1.0 / 16.0,
                in1=mask_sb[:, j, :],
                op0=ALU.mult,
                op1=ALU.subtract,
            )

        def rowmin(n):
            negm = st[("negm", n)]
            if pe_mask(n, 0):
                nc.vector.tensor_reduce(out=negm[:, 1:2], in_=st[("s2", n)][:, 1, :], axis=AX.X, op=ALU.min)
            else:
                nc.vector.tensor_reduce(out=negm[:], in_=st[("s2", n)][:], axis=AX.X, op=ALU.min)

        def expo(n, hh):
            if hh == 0:
                st[("e2", n)] = work.tile([P, H, S], BF16, tag="e2", name="e2")
                st[("rs", n)] = small.tile([P, H], F32, tag="rs", name="rs", bufs=5)
            nc.scalar.activation(
                out=st[("e2", n)][:, hh, :],
                in_=st[("s2", n)][:, hh, :],
                func=ACTF.Exp,
                bias=st[("negm", n)][:, hh:hh + 1],
                scale=-1.0,
                accum_out=st[("rs", n)][:, hh:hh + 1],
            )

        def e_t(n, hh):
            if hh == 0:
                st[("pe", n)] = ps_e.tile([P, NT, H, P], BF16, tag="pe", name="pe")
            pe = st[("pe", n)]
            e2 = st[("e2", n)]
            for t in range(NT):
                nc.tensor.transpose(
                    out=pe[:, t, hh, :],
                    in_=e2[:, hh, t * P:(t + 1) * P],
                    identity=ident_b[:],
                )

        def evac_t(n):
            epl = work.tile([P, NT, H * P], BF16, tag="epl", name="epl")
            nc.scalar.copy(
                out=epl[:].rearrange("p t c -> p (t c)"),
                in_=st[("pe", n)][:].rearrange("p t h c -> p (t h c)"),
            )
            st[("epl", n)] = epl

        def regroup(dst, src, eng):
            if eng == "pool":
                nc.gpsimd.tensor_scalar(
                    out=dst,
                    in0=src.rearrange("p t c -> p c t"),
                    scalar1=1.0,
                    scalar2=0.0,
                    op0=ALU.mult,
                    op1=ALU.add,
                )
            else:
                nc.vector.tensor_copy(
                    out=dst.rearrange("p (c i) t -> p c t i", i=4),
                    in_=src.rearrange("p t (c i) -> p c t i", i=4),
                )

        def regroup_e(n):
            grp = work.tile([P, H * P, NT], BF16, tag="grp", name="grp", bufs=3, align_bytes=64)
            regroup(grp[:], st[("epl", n)][:], E_REGROUP)
            st[("grp", n)] = grp

        def evac_regroup_e(n):
            grp = work.tile([P, H * P, NT], BF16, tag="grp", name="grp", bufs=3, align_bytes=64)
            nc.vector.tensor_copy(out=grp[:], in_=st[("pe", n)][:].rearrange("p t h c -> p (h c) t"))
            st[("grp", n)] = grp

        def quant_e(n):
            ec = work.tile([P, H * P], U32, tag="ec", name="ec", align_bytes=64)
            es = work.tile([P, H * P], U8, tag="es", name="es", align_bytes=64)
            nc.vector.quantize_mx(
                out=ec[:].bitcast(FP8X4),
                scales=es[:],
                in_=st[("grp", n)][:].rearrange("p c t -> p (c t)"),
            )
            rc = small.tile([P, H], F32, tag="rc", name="rc")
            nc.vector.reciprocal(out=rc[:], in_=st[("rs", n)][:])
            st[("ec", n)] = ec
            st[("es", n)] = es
            st[("rc", n)] = rc

        def regroup_v(b, r):
            if r == 0:
                st[("vgrp", b)] = work.tile([P, H * D, NT], BF16, tag="vgrp", name="vgrp", align_bytes=64)
            cs = slice(r * P, (r + 1) * P)
            regroup(st[("vgrp", b)][:, cs, :], st[("v_raw", b)][:, :, cs], V_REGROUP)

        def quant_v(b):
            vc = work.tile([P, H * D], U32, tag="vc", name="vc", align_bytes=64)
            vs = work.tile([P, H * D], U8, tag="vs", name="vs", align_bytes=64)
            nc.vector.quantize_mx(
                out=vc[:].bitcast(FP8X4),
                scales=vs[:],
                in_=st[("vgrp", b)][:].rearrange("p c t -> p (c t)"),
            )
            st[("vc", b)] = vc
            st[("vs", b)] = vs

        def pv(n):
            b, j = divmod(n, NT)
            if n >= NS - NLAST:
                po = ps_s.tile([P, H, D], F32, tag="s", name="po")
            else:
                po = ps_o.tile([P, H, D], F32, tag="po", name="po")
            for hh in range(H):
                nc.tensor.matmul_mx(
                    out=po[:, hh, :],
                    lhsT=st[("ec", n)][:, hh * P:(hh + 1) * P].bitcast(FP8X4),
                    lhsT_scale=st[("es", n)][:, hh * P:(hh + 1) * P],
                    rhs=st[("vc", b)][:, hh * D:(hh + 1) * D].bitcast(FP8X4),
                    rhs_scale=st[("vs", b)][:, hh * D:(hh + 1) * D],
                    start=True,
                    stop=True,
                )
            st[("po", n)] = po

        def o_evac(n):
            ob = work.tile([P, H, D], F32, tag="ob", name="ob", bufs=4)
            for hh in range(H):
                nc.scalar.activation(
                    out=ob[:, hh, :],
                    in_=st[("po", n)][:, hh, :],
                    func=ACTF.Copy,
                    scale=st[("rc", n)][:, hh:hh + 1],
                )
            st[("ob", n)] = ob

        def store(n):
            b, j = divmod(n, NT)
            nc.sync.dma_start(
                out=out[b].rearrange("(p j) h d -> p j (h d)", j=NT)[:, j, :],
                in_=st[("ob", n)][:].rearrange("p h d -> p (h d)"),
            )

        for r in range(4):
            prep_t(0, r, ps_s, "s")
        for r in range(4):
            prep_evac(0, r, "act" if r % 2 == 0 else "dve")

        def ok(n):
            return 0 <= n < NS

        def preps(c):
            if c in (0, 1):
                return [(1, 2 * c), (1, 2 * c + 1)]
            x = c + 2
            b1 = x // 4 + 1
            if c >= 2 and b1 < B:
                return [(b1, x % 4)]
            return []

        LAG = 3
        for c in range(-2, NS + LAG):
            pl = preps(c)
            for i, u in enumerate(pl):
                if i == 0:
                    prep_t(u[0], u[1], ps_t, "t")
                else:
                    prep_t(u[0], u[1], ps_o, "po")
            if ok(c + 2):
                qk(c + 2, 0)
            if ok(c + 1):
                stt(c + 1, 0)
            if ok(c - LAG):
                if (c - LAG) % NT == 0:
                    quant_v((c - LAG) // NT)
                quant_e(c - LAG)
                pv(c - LAG)
            if ok(c):
                expo(c, 0)
                e_t(c, 0)
            if ok(c - 1):
                if c - 1 >= NS - NLAST:
                    evac_regroup_e(c - 1)
                else:
                    evac_t(c - 1)
                    regroup_e(c - 1)
            xb, xr = divmod(c + 2, NT)
            if xb < B:
                regroup_v(xb, xr)
            if ok(c + 2):
                qk(c + 2, 1)
            if ok(c + 1):
                stt(c + 1, 1)
                rowmin(c + 1)
            if ok(c):
                expo(c, 1)
                e_t(c, 1)
            for u in pl:
                prep_evac(u[0], u[1], "act")
            if ok(c - LAG):
                o_evac(c - LAG)
                store(c - LAG)
            if (c + 2) % NT == 0:
                nb = (c + 2) // NT + 2
                if nb < B:
                    load_kq(nb)
                    load_v(nb)
